import numpy as np
import ml_dtypes


def mxq(x, axis, fmt="e4m3"):
    dtype, down = {"e4m3": (ml_dtypes.float8_e4m3fn, 7), "e5m2": (ml_dtypes.float8_e5m2, 14)}[fmt]
    v = np.moveaxis(np.asarray(x, np.float32).astype(ml_dtypes.bfloat16).astype(np.float64), axis, -1)
    blocks = v.reshape(v.shape[:-1] + (-1, 32))
    amax = np.abs(blocks).max(-1, keepdims=True)
    byte = np.maximum(np.where(amax > 0, np.frexp(amax)[1] - 1 + 127, 0) - down, 1)
    scale = np.exp2(byte - 127.0)
    codes = (blocks / scale).astype(np.float32).astype(dtype).astype(np.float64)
    return np.moveaxis((codes * scale).reshape(v.shape), -1, axis)


WIDE = False


def mx_kscale(k):
    if not WIDE:
        return np.ones(k)
    levels = np.array([10, -10, 5, -5, 0])
    a = np.random.permutation(np.resize(levels, k // 512 * 4)).reshape(k // 512, 4)
    idx = np.arange(k)
    return np.exp2(a[idx // 512, idx % 128 // 32])


BF16 = ml_dtypes.bfloat16


def bf(x):
    return np.asarray(x, np.float32).astype(BF16)


def f64(x):
    return np.asarray(x).astype(np.float64)


E2M1 = np.array([0.0, 0.5, 1.0, 1.5, 2.0, 3.0, 4.0, 6.0, -0.0, -0.5, -1.0, -1.5, -2.0, -3.0, -4.0, -6.0])


def pack_weight(w, fmt):
    k, n = w.shape
    w = f64(bf(w)).reshape(k // 32, 32, n)
    amax = np.abs(w).max(1)
    if fmt == "e4m3":
        byte = np.frexp(amax)[1] - 1 + 127 - 7
    else:
        mant, ex = np.frexp(amax / 6.0)
        byte = np.where(mant > 0.5, ex, ex - 1) + 127
    byte = np.clip(np.where(amax > 0, byte, 1), 1, 254)
    scaled = (w * np.exp2(127.0 - byte)[:, None, :]).reshape(k, n).astype(np.float32)
    by_word = np.ascontiguousarray(scaled.reshape(k // 512, 128, 4, n).transpose(0, 1, 3, 2))
    if fmt == "e4m3":
        words = by_word.astype(ml_dtypes.float8_e4m3fn).view(np.uint8)
    else:
        c = by_word.astype(ml_dtypes.float4_e2m1fn).view(np.uint8) & 0xF
        words = c[..., 0::2] | (c[..., 1::2] << 4)
    return np.ascontiguousarray(words), np.ascontiguousarray(byte.astype(np.uint8).reshape(k // 512, 16, n))


def unpack_weight(words, scales, fmt):
    g, p, n, _ = words.shape
    if fmt == "e4m3":
        vals = np.ascontiguousarray(words).view(ml_dtypes.float8_e4m3fn).astype(np.float64)
    else:
        nib = np.empty((g, p, n, 4), np.uint8)
        nib[..., 0::2] = words & 0xF
        nib[..., 1::2] = words >> 4
        vals = E2M1[nib]
    vals = vals * np.repeat(np.exp2(scales.astype(np.float64) - 127.0), 8, axis=1)[..., None]
    return vals.transpose(0, 1, 3, 2).reshape(g * 512, n)

def pack4(w):
    words, scales = pack_weight(w, "e2m1")
    return words.reshape(words.shape[0], 128, -1), scales


def unpack4(words, scales):
    return unpack_weight(words.reshape(words.shape[0], 128, -1, 2), scales, "e2m1")


B, D, H = 4096, 1024, 256


def sigmoid(v):
    return 1.0 / (1.0 + np.exp(-v))


def setup_inputs():
    s = mx_kscale(D)
    x = bf(np.random.standard_normal((B, D)) * s)
    w = np.random.standard_normal((4 * H, D)) * 1.5 / np.sqrt(D) / s[None, :]
    words, scales = pack4(np.ascontiguousarray(w.T))
    b_ih0 = bf(np.random.standard_normal(4 * H) * 0.3)
    b_hh0 = bf(np.random.standard_normal(4 * H) * 0.3)
    return {"x": x,
            "W_ih0_words": words,
            "W_ih0_scales": scales,
            "b_ih0": b_ih0,
            "b_hh0": b_hh0}


def reference(x, W_ih0_words, W_ih0_scales, b_ih0, b_hh0):
    wt = unpack4(W_ih0_words, W_ih0_scales)
    b = f64(b_ih0) + f64(b_hh0)
    xq = mxq(f64(x), 1, "e4m3")
    a_i = (xq @ wt[:, :H]) + b[:H]
    a_go = (xq @ wt[:, 2 * H:]) + b[2 * H:]
    a_g, a_o = a_go[:, :H], a_go[:, H:]
    c = sigmoid(a_i) * np.tanh(a_g)
    return sigmoid(a_o) * np.tanh(c)

@@ -1,0 +1,192 @@
+from contextlib import ExitStack
+
+import concourse.mybir as mybir
+from concourse.masks import make_identity
+
+F32 = mybir.dt.float32
+BF16 = mybir.dt.bfloat16
+I32 = mybir.dt.int32
+U32 = mybir.dt.uint32
+U8 = mybir.dt.uint8
+FP8X4 = mybir.dt.float8_e4m3fn_x4
+FP4X4 = mybir.dt.float4_e2m1fn_x4
+ACT = mybir.ActivationFunctionType
+ALU = mybir.AluOpType
+
+B, D, H = 4096, 1024, 256
+P = 128
+PACK = 4
+K_PASS = P * PACK
+PASSES = D // K_PASS
+WORDS = K_PASS // 2
+ROW_TILES = B // P
+GROUP_ROWS = 512
+GROUP_TILES = GROUP_ROWS // P
+GROUPS = B // GROUP_ROWS
+PAIR_ROWS = 2 * P
+PAIRS = GROUP_ROWS // PAIR_ROWS
+HALVES = H // P
+STEPS = GROUPS * HALVES
+assert PAIRS == HALVES
+GATES_IN_W = 4
+COLUMN_TILES = GATES_IN_W * HALVES
+GATE_I, GATE_G, GATE_O = 0, 2, 3
+
+FLOPS = 2 * B * D * 3 * H
+BYTES = B * D * 2 + B * H * 4 + 3 * H * D // 2 + 3 * H * D // 32 + 2 * 3 * H * 2
+
+
+def tile_lstmbaseline_pa_t_kernel(tc, x, w_words, w_scales, b_ih0, b_hh0, out):
+    nc = tc.nc
+    x_rows = x.rearrange("(p t) k -> p t k", t=ROW_TILES)
+    out_rows = out.rearrange("(p t) c -> p t c", t=ROW_TILES)
+
+    with ExitStack() as stack:
+        stack.enter_context(tc.manual_schedule())
+        keep = stack.enter_context(tc.tile_pool(name="keep", bufs=1))
+        two = stack.enter_context(tc.tile_pool(name="two", bufs=2))
+        xt_banks = stack.enter_context(tc.psum_pool(name="xt_banks", bufs=3))
+        mx_banks = stack.enter_context(tc.psum_pool(name="mx_banks", bufs=3))
+        ot_banks = stack.enter_context(tc.psum_pool(name="ot_banks", bufs=2))
+
+        bias_rows = keep.tile([P, P], BF16, name="bias_rows")
+        nc.vector.memset(bias_rows[:], 0.0)
+        nc.scalar.dma_start(out=bias_rows[0:COLUMN_TILES, :], in_=b_ih0.rearrange("(j c) -> j c", c=P))
+        nc.scalar.dma_start(
+            out=bias_rows[COLUMN_TILES : 2 * COLUMN_TILES, :], in_=b_hh0.rearrange("(j c) -> j c", c=P)
+        )
+
+        x_sb = []
+        for w in range(GROUPS * PAIRS):
+            x_sb.append(keep.tile([P, 2, D], BF16, name="x%d" % w))
+
+        def load_x(w):
+            nc.sync.dma_start(out=x_sb[w][:], in_=x_rows[:, 2 * w : 2 * (w + 1), :])
+
+        for w in range(PAIRS):
+            load_x(w)
+        w_planes = keep.tile([P, PASSES, GATES_IN_W * H], U8, name="w_planes", align_bytes=64)
+        nc.vector.memset(w_planes[:].bitcast(I32), 0)
+        for quadrant in range(4):
+            nc.sync.dma_start(
+                out=w_planes[32 * quadrant : 32 * quadrant + 4, :, :].bitcast(I32),
+                in_=w_scales[:, 4 * quadrant : 4 * quadrant + 4, :].rearrange("g r n -> r g n").bitcast(I32),
+            )
+        w_codes = keep.tile([P, PASSES, 2 * GATES_IN_W * H], U8, name="w_codes", align_bytes=64)
+        nc.sync.dma_start(out=w_codes[:].bitcast(I32), in_=w_words.rearrange("g p n -> p g n").bitcast(I32))
+        for w in range(PAIRS, GROUPS * PAIRS):
+            load_x(w)
+
+        ident_f32 = keep.tile([P, P], F32, name="ident_f32")
+        make_identity(nc, ident_f32[:])
+        ident_bf16 = keep.tile([P, P], BF16, name="ident_bf16")
+        nc.vector.tensor_copy(out=ident_bf16[:], in_=ident_f32[:])
+
+        warm = keep.tile([P, 1], F32, name="warm")
+        nc.vector.memset(warm[:], 0.0)
+        nc.scalar.activation(out=warm[:], in_=warm[:], func=ACT.Sigmoid)
+
+        bias = keep.tile([P, COLUMN_TILES], F32, name="bias")
+
+        def prepare_bias():
+            bias_ps = ot_banks.tile([P, P], BF16, name="bias_ps", tag="ot")
+            nc.tensor.transpose(bias_ps[:], bias_rows[:], ident_bf16[:])
+            bias_parts = keep.tile([P, 2 * COLUMN_TILES], F32, name="bias_parts")
+            nc.vector.tensor_copy(out=bias_parts[:], in_=bias_ps[:, 0 : 2 * COLUMN_TILES])
+            nc.vector.tensor_tensor(
+                out=bias[:], in0=bias_parts[:, 0:COLUMN_TILES], in1=bias_parts[:, COLUMN_TILES:], op=ALU.add
+            )
+
+        grouped, x_codes, x_planes = {}, {}, {}
+        gates, cell, cell_tanh, hidden, out_sb = {}, {}, {}, {}, {}
+
+        def transpose_x(w):
+            grouped[w] = two.tile([P, PASSES, PAIR_ROWS, PACK], BF16, name="grouped%d" % w, tag="grouped", align_bytes=64)
+            for g in range(PASSES):
+                bank = xt_banks.tile([P, 2, PAIR_ROWS], F32, name="xt%d_%d" % (w, g), tag="xt")
+                for u in range(2):
+                    for i in range(2):
+                        nc.tensor.transpose(
+                            bank[:, u, i * P : (i + 1) * P],
+                            x_sb[w][:, i, :].bitcast(F32)[:, g * WORDS + u : (g + 1) * WORDS : 2],
+                            ident_f32[:],
+                        )
+                nc.vector.tensor_copy(
+                    out=grouped[w][:, g, :, :].bitcast(F32), in_=bank[:].rearrange("p u r -> p r u")
+                )
+
+        def quantise_x(w):
+            j, pair = divmod(w, PAIRS)
+            if pair == 0:
+                x_codes[j] = two.tile([P, PASSES, GROUP_ROWS], U32, name="x_codes%d" % j, tag="x_codes", align_bytes=64)
+                x_planes[j] = two.tile([P, PASSES, GROUP_ROWS], U8, name="x_planes%d" % j, tag="x_planes", align_bytes=64)
+            rows = slice(pair * PAIR_ROWS, (pair + 1) * PAIR_ROWS)
+            for g in range(PASSES):
+                nc.vector.quantize_mx(
+                    out=x_codes[j][:, g, rows].bitcast(FP8X4),
+                    scales=x_planes[j][:, g, rows],
+                    in_=grouped[w][:, g, :, :].rearrange("p r t -> p (r t)"),
+                )
+
+        def gate_products(v):
+            j, h = divmod(v, HALVES)
+            gates[v] = {}
+            for gate in (GATE_I, GATE_G, GATE_O):
+                c = gate * HALVES + h
+                acc = mx_banks.tile([P, GROUP_ROWS], F32, name="acc%d_%d" % (v, gate), tag="acc")
+                for g in range(PASSES):
+                    nc.tensor.matmul_mx(
+                        out=acc[:],
+                        lhsT=w_codes[:, g, 2 * c * P : 2 * (c + 1) * P].bitcast(FP4X4),
+                        lhsT_scale=w_planes[:, g, c * P : (c + 1) * P],
+                        rhs=x_codes[j][:, g, :].bitcast(FP8X4),
+                        rhs_scale=x_planes[j][:, g, :],
+                        start=(g == 0),
+                        stop=(g == PASSES - 1),
+                    )
+                gates[v][gate] = two.tile([P, GROUP_ROWS], F32, name="gate%d_%d" % (gate, v), tag="gate%d" % gate)
+                nc.scalar.activation(
+                    out=gates[v][gate][:],
+                    in_=acc[:],
+                    func=ACT.Tanh if gate == GATE_G else ACT.Sigmoid,
+                    bias=bias[:, c : c + 1],
+                )
+
+        def cell_state(v):
+            cell[v] = two.tile([P, GROUP_ROWS], F32, name="cell%d" % v, tag="cell")
+            nc.vector.tensor_tensor(out=cell[v][:], in0=gates[v][GATE_I][:], in1=gates[v][GATE_G][:], op=ALU.mult)
+
+        def tanh_of_cell(v):
+            cell_tanh[v] = two.tile([P, GROUP_ROWS], F32, name="cell_tanh%d" % v, tag="cell_tanh")
+            nc.scalar.activation(out=cell_tanh[v][:], in_=cell[v][:], func=ACT.Tanh)
+
+        def hidden_state(v):
+            hidden[v] = two.tile([P, GROUP_ROWS], F32, name="hidden%d" % v, tag="hidden")
+            nc.vector.tensor_tensor(out=hidden[v][:], in0=gates[v][GATE_O][:], in1=cell_tanh[v][:], op=ALU.mult)
+
+        def store(v):
+            j, h = divmod(v, HALVES)
+            if h == 0:
+                out_sb[j] = keep.tile([P, GROUP_TILES, H], F32, name="out_sb%d" % j)
+            bank = ot_banks.tile([P, GROUP_TILES, P], F32, name="ot%d" % v, tag="ot")
+            for t in range(GROUP_TILES):
+                nc.tensor.transpose(bank[:, t, :], hidden[v][:, t * P : (t + 1) * P], ident_f32[:])
+            nc.scalar.copy(out=out_sb[j][:, :, h * P : (h + 1) * P], in_=bank[:])
+            if h == HALVES - 1:
+                nc.sync.dma_start(out=out_rows[:, j * GROUP_TILES : (j + 1) * GROUP_TILES, :], in_=out_sb[j][:])
+
+        def when(index, stage):
+            if 0 <= index < STEPS:
+                stage(index)
+
+        transpose_x(0)
+        quantise_x(0)
+        prepare_bias()
+        for v in range(-1, STEPS + 2):
+            when(v - 1, tanh_of_cell)
+            when(v + 2, transpose_x)
+            when(v - 1, hidden_state)
+            when(v - 2, store)
+            when(v + 2, quantise_x)
+            when(v, gate_products)
+            when(v, cell_state)

@@ -45,6 +45,7 @@ def tile_lstmbaseline_pa_t_kernel(tc, x, w_words, w_scales, b_ih0, b_hh0, out):
         stack.enter_context(tc.manual_schedule())
         keep = stack.enter_context(tc.tile_pool(name="keep", bufs=1))
         two = stack.enter_context(tc.tile_pool(name="two", bufs=2))
+        three = stack.enter_context(tc.tile_pool(name="three", bufs=3))
         xt_banks = stack.enter_context(tc.psum_pool(name="xt_banks", bufs=3))
         mx_banks = stack.enter_context(tc.psum_pool(name="mx_banks", bufs=3))
         ot_banks = stack.enter_context(tc.psum_pool(name="ot_banks", bufs=2))
@@ -111,9 +112,8 @@ def tile_lstmbaseline_pa_t_kernel(tc, x, w_words, w_scales, b_ih0, b_hh0, out):
                             x_sb[w][:, i, :].bitcast(F32)[:, g * WORDS + u : (g + 1) * WORDS : 2],
                             ident_f32[:],
                         )
-                nc.vector.tensor_copy(
-                    out=grouped[w][:, g, :, :].bitcast(F32), in_=bank[:].rearrange("p u r -> p r u")
-                )
+                copy_out = nc.vector.tensor_copy if g == 0 else nc.scalar.copy
+                copy_out(out=grouped[w][:, g, :, :].bitcast(F32), in_=bank[:].rearrange("p u r -> p r u"))
 
         def quantise_x(w):
             j, pair = divmod(w, PAIRS)
@@ -128,41 +128,39 @@ def tile_lstmbaseline_pa_t_kernel(tc, x, w_words, w_scales, b_ih0, b_hh0, out):
                     in_=grouped[w][:, g, :, :].rearrange("p r t -> p (r t)"),
                 )
 
-        def gate_products(v):
+        def gate(v, which):
             j, h = divmod(v, HALVES)
-            gates[v] = {}
-            for gate in (GATE_I, GATE_G, GATE_O):
-                c = gate * HALVES + h
-                acc = mx_banks.tile([P, GROUP_ROWS], F32, name="acc%d_%d" % (v, gate), tag="acc")
-                for g in range(PASSES):
-                    nc.tensor.matmul_mx(
-                        out=acc[:],
-                        lhsT=w_codes[:, g, 2 * c * P : 2 * (c + 1) * P].bitcast(FP4X4),
-                        lhsT_scale=w_planes[:, g, c * P : (c + 1) * P],
-                        rhs=x_codes[j][:, g, :].bitcast(FP8X4),
-                        rhs_scale=x_planes[j][:, g, :],
-                        start=(g == 0),
-                        stop=(g == PASSES - 1),
-                    )
-                gates[v][gate] = two.tile([P, GROUP_ROWS], F32, name="gate%d_%d" % (gate, v), tag="gate%d" % gate)
-                nc.scalar.activation(
-                    out=gates[v][gate][:],
-                    in_=acc[:],
-                    func=ACT.Tanh if gate == GATE_G else ACT.Sigmoid,
-                    bias=bias[:, c : c + 1],
+            c = which * HALVES + h
+            acc = mx_banks.tile([P, GROUP_ROWS], F32, name="acc%d_%d" % (v, which), tag="acc")
+            for g in range(PASSES):
+                nc.tensor.matmul_mx(
+                    out=acc[:],
+                    lhsT=w_codes[:, g, 2 * c * P : 2 * (c + 1) * P].bitcast(FP4X4),
+                    lhsT_scale=w_planes[:, g, c * P : (c + 1) * P],
+                    rhs=x_codes[j][:, g, :].bitcast(FP8X4),
+                    rhs_scale=x_planes[j][:, g, :],
+                    start=(g == 0),
+                    stop=(g == PASSES - 1),
                 )
+            gates[v, which] = two.tile([P, GROUP_ROWS], F32, name="gate%d_%d" % (which, v), tag="gate%d" % which)
+            nc.scalar.activation(
+                out=gates[v, which][:],
+                in_=acc[:],
+                func=ACT.Tanh if which == GATE_G else ACT.Sigmoid,
+                bias=bias[:, c : c + 1],
+            )
 
         def cell_state(v):
             cell[v] = two.tile([P, GROUP_ROWS], F32, name="cell%d" % v, tag="cell")
-            nc.vector.tensor_tensor(out=cell[v][:], in0=gates[v][GATE_I][:], in1=gates[v][GATE_G][:], op=ALU.mult)
+            nc.vector.tensor_tensor(out=cell[v][:], in0=gates[v, GATE_I][:], in1=gates[v, GATE_G][:], op=ALU.mult)
 
         def tanh_of_cell(v):
             cell_tanh[v] = two.tile([P, GROUP_ROWS], F32, name="cell_tanh%d" % v, tag="cell_tanh")
             nc.scalar.activation(out=cell_tanh[v][:], in_=cell[v][:], func=ACT.Tanh)
 
         def hidden_state(v):
-            hidden[v] = two.tile([P, GROUP_ROWS], F32, name="hidden%d" % v, tag="hidden")
-            nc.vector.tensor_tensor(out=hidden[v][:], in0=gates[v][GATE_O][:], in1=cell_tanh[v][:], op=ALU.mult)
+            hidden[v] = three.tile([P, GROUP_ROWS], F32, name="hidden%d" % v, tag="hidden")
+            nc.vector.tensor_tensor(out=hidden[v][:], in0=gates[v, GATE_O][:], in1=cell_tanh[v][:], op=ALU.mult)
 
         def store(v):
             j, h = divmod(v, HALVES)
@@ -171,22 +169,24 @@ def tile_lstmbaseline_pa_t_kernel(tc, x, w_words, w_scales, b_ih0, b_hh0, out):
             bank = ot_banks.tile([P, GROUP_TILES, P], F32, name="ot%d" % v, tag="ot")
             for t in range(GROUP_TILES):
                 nc.tensor.transpose(bank[:, t, :], hidden[v][:, t * P : (t + 1) * P], ident_f32[:])
-            nc.scalar.copy(out=out_sb[j][:, :, h * P : (h + 1) * P], in_=bank[:])
+            nc.vector.tensor_copy(out=out_sb[j][:, :, h * P : (h + 1) * P], in_=bank[:])
             if h == HALVES - 1:
                 nc.sync.dma_start(out=out_rows[:, j * GROUP_TILES : (j + 1) * GROUP_TILES, :], in_=out_sb[j][:])
 
-        def when(index, stage):
+        def when(index, stage, *args):
             if 0 <= index < STEPS:
-                stage(index)
+                stage(index, *args)
 
         transpose_x(0)
         quantise_x(0)
         prepare_bias()
-        for v in range(-1, STEPS + 2):
-            when(v - 1, tanh_of_cell)
+        for v in range(-1, STEPS + 3):
             when(v + 2, transpose_x)
-            when(v - 1, hidden_state)
-            when(v - 2, store)
+            when(v - 3, store)
             when(v + 2, quantise_x)
-            when(v, gate_products)
+            when(v, gate, GATE_I)
+            when(v, gate, GATE_G)
             when(v, cell_state)
+            when(v - 1, tanh_of_cell)
+            when(v, gate, GATE_O)
+            when(v - 1, hidden_state)

@@ -31,6 +31,10 @@ assert PAIRS == HALVES
 GATES_IN_W = 4
 COLUMN_TILES = GATES_IN_W * HALVES
 GATE_I, GATE_G, GATE_O = 0, 2, 3
+BLOCK = 32
+QUADRANTS = P // BLOCK
+ROW_BLOCKS = GROUP_ROWS // BLOCK
+RUN = HALVES * BLOCK
 
 FLOPS = 2 * B * D * 3 * H
 BYTES = B * D * 2 + B * H * 4 + 3 * H * D // 2 + 3 * H * D // 32 + 2 * 3 * H * 2
@@ -38,24 +42,27 @@ BYTES = B * D * 2 + B * H * 4 + 3 * H * D // 2 + 3 * H * D // 32 + 2 * 3 * H * 2
 
 def tile_lstmbaseline_pa_t_kernel(tc, x, w_words, w_scales, b_ih0, b_hh0, out):
     nc = tc.nc
-    x_rows = x.rearrange("(p t) k -> p t k", t=ROW_TILES)
-    out_rows = out.rearrange("(p t) c -> p t c", t=ROW_TILES)
+    x_rows = x.rearrange("(t p) k -> p t k", p=P)
+    out_runs = out.rearrange("(j s a) (i e) -> j i a s e", s=ROW_BLOCKS, a=BLOCK, e=RUN)
 
     with ExitStack() as stack:
         stack.enter_context(tc.manual_schedule())
         keep = stack.enter_context(tc.tile_pool(name="keep", bufs=1))
         two = stack.enter_context(tc.tile_pool(name="two", bufs=2))
         three = stack.enter_context(tc.tile_pool(name="three", bufs=3))
-        xt_banks = stack.enter_context(tc.psum_pool(name="xt_banks", bufs=3))
-        mx_banks = stack.enter_context(tc.psum_pool(name="mx_banks", bufs=3))
-        ot_banks = stack.enter_context(tc.psum_pool(name="ot_banks", bufs=2))
+        xt_banks = stack.enter_context(tc.psum_pool(name="xt_banks", bufs=4))
+        mx_banks = stack.enter_context(tc.psum_pool(name="mx_banks", bufs=4))
 
         bias_rows = keep.tile([P, P], BF16, name="bias_rows")
         nc.vector.memset(bias_rows[:], 0.0)
-        nc.scalar.dma_start(out=bias_rows[0:COLUMN_TILES, :], in_=b_ih0.rearrange("(j c) -> j c", c=P))
-        nc.scalar.dma_start(
-            out=bias_rows[COLUMN_TILES : 2 * COLUMN_TILES, :], in_=b_hh0.rearrange("(j c) -> j c", c=P)
-        )
+        for first_row, vector in ((0, b_ih0), (COLUMN_TILES, b_hh0)):
+            for h in range(HALVES):
+                nc.scalar.dma_start(
+                    out=bias_rows[first_row + h : first_row + COLUMN_TILES : HALVES, :].rearrange(
+                        "G (i b) -> G i b", b=BLOCK
+                    ),
+                    in_=vector.rearrange("(G i h b) -> h G i b", i=QUADRANTS, h=HALVES, b=BLOCK)[h],
+                )
 
         x_sb = []
         for w in range(GROUPS * PAIRS):
@@ -66,15 +73,15 @@ def tile_lstmbaseline_pa_t_kernel(tc, x, w_words, w_scales, b_ih0, b_hh0, out):
 
         for w in range(PAIRS):
             load_x(w)
-        w_planes = keep.tile([P, PASSES, GATES_IN_W * H], U8, name="w_planes", align_bytes=64)
-        nc.vector.memset(w_planes[:].bitcast(I32), 0)
+        w_planes_in = keep.tile([P, PASSES, GATES_IN_W * H], U8, name="w_planes_in", align_bytes=64)
+        nc.vector.memset(w_planes_in[:].bitcast(I32), 0)
         for quadrant in range(4):
             nc.sync.dma_start(
-                out=w_planes[32 * quadrant : 32 * quadrant + 4, :, :].bitcast(I32),
+                out=w_planes_in[32 * quadrant : 32 * quadrant + 4, :, :].bitcast(I32),
                 in_=w_scales[:, 4 * quadrant : 4 * quadrant + 4, :].rearrange("g r n -> r g n").bitcast(I32),
             )
-        w_codes = keep.tile([P, PASSES, 2 * GATES_IN_W * H], U8, name="w_codes", align_bytes=64)
-        nc.sync.dma_start(out=w_codes[:].bitcast(I32), in_=w_words.rearrange("g p n -> p g n").bitcast(I32))
+        w_codes_in = keep.tile([P, PASSES, 2 * GATES_IN_W * H], U8, name="w_codes_in", align_bytes=64)
+        nc.sync.dma_start(out=w_codes_in[:].bitcast(I32), in_=w_words.rearrange("g p n -> p g n").bitcast(I32))
         for w in range(PAIRS, GROUPS * PAIRS):
             load_x(w)
 
@@ -87,10 +94,25 @@ def tile_lstmbaseline_pa_t_kernel(tc, x, w_words, w_scales, b_ih0, b_hh0, out):
         nc.vector.memset(warm[:], 0.0)
         nc.scalar.activation(out=warm[:], in_=warm[:], func=ACT.Sigmoid)
 
+        w_codes = keep.tile([P, PASSES, 2 * GATES_IN_W * H], U8, name="w_codes", align_bytes=64)
+        w_planes = keep.tile([P, PASSES, GATES_IN_W * H], U8, name="w_planes", align_bytes=64)
+
+        def order_w_columns():
+            for ordered, arrived in ((w_planes, w_planes_in), (w_codes, w_codes_in)):
+                for h in range(HALVES):
+                    nc.vector.tensor_copy(
+                        out=ordered[:].bitcast(I32).rearrange(
+                            "p g (G h i w) -> p (g G) h i w", G=GATES_IN_W, h=HALVES, i=QUADRANTS
+                        )[:, :, h, :, :],
+                        in_=arrived[:].bitcast(I32).rearrange(
+                            "p g (G i h w) -> p (g G) i h w", G=GATES_IN_W, h=HALVES, i=QUADRANTS
+                        )[:, :, :, h, :],
+                    )
+
         bias = keep.tile([P, COLUMN_TILES], F32, name="bias")
 
         def prepare_bias():
-            bias_ps = ot_banks.tile([P, P], BF16, name="bias_ps", tag="ot")
+            bias_ps = xt_banks.tile([P, P], BF16, name="bias_ps", tag="xt")
             nc.tensor.transpose(bias_ps[:], bias_rows[:], ident_bf16[:])
             bias_parts = keep.tile([P, 2 * COLUMN_TILES], F32, name="bias_parts")
             nc.vector.tensor_copy(out=bias_parts[:], in_=bias_ps[:, 0 : 2 * COLUMN_TILES])
@@ -99,7 +121,7 @@ def tile_lstmbaseline_pa_t_kernel(tc, x, w_words, w_scales, b_ih0, b_hh0, out):
             )
 
         grouped, x_codes, x_planes = {}, {}, {}
-        gates, cell, cell_tanh, hidden, out_sb = {}, {}, {}, {}, {}
+        gates, cell, cell_tanh, hidden, turned = {}, {}, {}, {}, {}
 
         def transpose_x(w):
             grouped[w] = two.tile([P, PASSES, PAIR_ROWS, PACK], BF16, name="grouped%d" % w, tag="grouped", align_bytes=64)
@@ -159,19 +181,30 @@ def tile_lstmbaseline_pa_t_kernel(tc, x, w_words, w_scales, b_ih0, b_hh0, out):
             nc.scalar.activation(out=cell_tanh[v][:], in_=cell[v][:], func=ACT.Tanh)
 
         def hidden_state(v):
-            hidden[v] = three.tile([P, GROUP_ROWS], F32, name="hidden%d" % v, tag="hidden")
-            nc.vector.tensor_tensor(out=hidden[v][:], in0=gates[v, GATE_O][:], in1=cell_tanh[v][:], op=ALU.mult)
-
-        def store(v):
             j, h = divmod(v, HALVES)
             if h == 0:
-                out_sb[j] = keep.tile([P, GROUP_TILES, H], F32, name="out_sb%d" % j)
-            bank = ot_banks.tile([P, GROUP_TILES, P], F32, name="ot%d" % v, tag="ot")
-            for t in range(GROUP_TILES):
-                nc.tensor.transpose(bank[:, t, :], hidden[v][:, t * P : (t + 1) * P], ident_f32[:])
-            nc.vector.tensor_copy(out=out_sb[j][:, :, h * P : (h + 1) * P], in_=bank[:])
-            if h == HALVES - 1:
-                nc.sync.dma_start(out=out_rows[:, j * GROUP_TILES : (j + 1) * GROUP_TILES, :], in_=out_sb[j][:])
+                hidden[j] = three.tile([P, ROW_BLOCKS, HALVES, BLOCK], F32, name="hidden%d" % j, tag="hidden", align_bytes=64)
+            nc.vector.tensor_tensor(
+                out=hidden[j][:, :, h, :],
+                in0=gates[v, GATE_O][:].rearrange("p (s a) -> p s a", a=BLOCK),
+                in1=cell_tanh[v][:].rearrange("p (s a) -> p s a", a=BLOCK),
+                op=ALU.mult,
+            )
+
+        def store(piece):
+            j, part = divmod(piece, 2)
+            blocks = ROW_BLOCKS // 2
+            width = blocks * RUN
+            turned[piece] = three.tile([P, width], F32, name="turned%d" % piece, tag="turned", align_bytes=64)
+            nc.vector.transpose(
+                out=turned[piece][:],
+                in_=hidden[j][:].rearrange("p s h a -> p (s h a)")[:, part * width : (part + 1) * width],
+            )
+            for i in range(QUADRANTS):
+                nc.sync.dma_start(
+                    out=out_runs[j, i, :, part * blocks : (part + 1) * blocks, :],
+                    in_=turned[piece][i * BLOCK : (i + 1) * BLOCK, :].rearrange("a (s e) -> a s e", e=RUN),
+                )
 
         def when(index, stage, *args):
             if 0 <= index < STEPS:
@@ -184,6 +217,8 @@ def tile_lstmbaseline_pa_t_kernel(tc, x, w_words, w_scales, b_ih0, b_hh0, out):
             when(v + 2, transpose_x)
             when(v - 3, store)
             when(v + 2, quantise_x)
+            if v == -1:
+                order_w_columns()
             when(v, gate, GATE_I)
             when(v, gate, GATE_G)
             when(v, cell_state)

@@ -36,6 +36,10 @@ QUADRANTS = P // BLOCK
 ROW_BLOCKS = GROUP_ROWS // BLOCK
 RUN = HALVES * BLOCK
 
+WARM_UP = 5
+WAIT_FOR_W = 4
+ON_GPSIMD = 12
+
 FLOPS = 2 * B * D * 3 * H
 BYTES = B * D * 2 + B * H * 4 + 3 * H * D // 2 + 3 * H * D // 32 + 2 * 3 * H * 2
 
@@ -52,6 +56,17 @@ def tile_lstmbaseline_pa_t_kernel(tc, x, w_words, w_scales, b_ih0, b_hh0, out):
         three = stack.enter_context(tc.tile_pool(name="three", bufs=3))
         xt_banks = stack.enter_context(tc.psum_pool(name="xt_banks", bufs=4))
         mx_banks = stack.enter_context(tc.psum_pool(name="mx_banks", bufs=4))
+
+        idle_operand = keep.tile([P, GROUP_ROWS], BF16, name="idle_operand")
+        nc.vector.memset(idle_operand[:], 0.0)
+        unread = []
+
+        def keep_clock_up(count):
+            for n in range(count):
+                unread.append(mx_banks.tile([P, GROUP_ROWS], F32, name="unread%d" % len(unread), tag="acc"))
+                nc.tensor.matmul(out=unread[-1][:], lhsT=idle_operand[:, 0:P], rhs=idle_operand[:], start=True, stop=True)
+
+        keep_clock_up(WARM_UP)
 
         bias_rows = keep.tile([P, P], BF16, name="bias_rows")
         nc.vector.memset(bias_rows[:], 0.0)
@@ -94,20 +109,19 @@ def tile_lstmbaseline_pa_t_kernel(tc, x, w_words, w_scales, b_ih0, b_hh0, out):
         nc.vector.memset(warm[:], 0.0)
         nc.scalar.activation(out=warm[:], in_=warm[:], func=ACT.Sigmoid)
 
-        w_codes = keep.tile([P, PASSES, 2 * GATES_IN_W * H], U8, name="w_codes", align_bytes=64)
-        w_planes = keep.tile([P, PASSES, GATES_IN_W * H], U8, name="w_planes", align_bytes=64)
+        w_codes, w_planes = [], []
+        for h in range(HALVES):
+            w_codes.append(keep.tile([P, PASSES, 2 * GATES_IN_W * P], U8, name="w_codes%d" % h, align_bytes=64))
+            w_planes.append(keep.tile([P, PASSES, GATES_IN_W * P], U8, name="w_planes%d" % h, align_bytes=64))
 
-        def order_w_columns():
-            for ordered, arrived in ((w_planes, w_planes_in), (w_codes, w_codes_in)):
-                for h in range(HALVES):
-                    nc.vector.tensor_copy(
-                        out=ordered[:].bitcast(I32).rearrange(
-                            "p g (G h i w) -> p (g G) h i w", G=GATES_IN_W, h=HALVES, i=QUADRANTS
-                        )[:, :, h, :, :],
-                        in_=arrived[:].bitcast(I32).rearrange(
-                            "p g (G i h w) -> p (g G) i h w", G=GATES_IN_W, h=HALVES, i=QUADRANTS
-                        )[:, :, :, h, :],
-                    )
+        def order_w_columns(h):
+            for ordered, arrived in ((w_planes[h], w_planes_in), (w_codes[h], w_codes_in)):
+                nc.vector.tensor_copy(
+                    out=ordered[:].bitcast(I32).rearrange("p g (G i w) -> p (g G) i w", G=GATES_IN_W, i=QUADRANTS),
+                    in_=arrived[:].bitcast(I32).rearrange(
+                        "p g (G i h w) -> p (g G) i h w", G=GATES_IN_W, h=HALVES, i=QUADRANTS
+                    )[:, :, :, h, :],
+                )
 
         bias = keep.tile([P, COLUMN_TILES], F32, name="bias")
 
@@ -124,7 +138,7 @@ def tile_lstmbaseline_pa_t_kernel(tc, x, w_words, w_scales, b_ih0, b_hh0, out):
         gates, cell, cell_tanh, hidden, turned = {}, {}, {}, {}, {}
 
         def transpose_x(w):
-            grouped[w] = two.tile([P, PASSES, PAIR_ROWS, PACK], BF16, name="grouped%d" % w, tag="grouped", align_bytes=64)
+            grouped[w] = three.tile([P, PASSES, PAIR_ROWS, PACK], BF16, name="grouped%d" % w, tag="grouped", align_bytes=64)
             for g in range(PASSES):
                 bank = xt_banks.tile([P, 2, PAIR_ROWS], F32, name="xt%d_%d" % (w, g), tag="xt")
                 for u in range(2):
@@ -134,14 +148,16 @@ def tile_lstmbaseline_pa_t_kernel(tc, x, w_words, w_scales, b_ih0, b_hh0, out):
                             x_sb[w][:, i, :].bitcast(F32)[:, g * WORDS + u : (g + 1) * WORDS : 2],
                             ident_f32[:],
                         )
-                copy_out = nc.vector.tensor_copy if g == 0 else nc.scalar.copy
+                copy_out = nc.scalar.copy if (w < PAIRS or (g == 1 and w % 2 == 0)) else nc.vector.tensor_copy
                 copy_out(out=grouped[w][:, g, :, :].bitcast(F32), in_=bank[:].rearrange("p u r -> p r u"))
+                if w < PAIRS:
+                    keep_clock_up(1)
 
         def quantise_x(w):
             j, pair = divmod(w, PAIRS)
             if pair == 0:
-                x_codes[j] = two.tile([P, PASSES, GROUP_ROWS], U32, name="x_codes%d" % j, tag="x_codes", align_bytes=64)
-                x_planes[j] = two.tile([P, PASSES, GROUP_ROWS], U8, name="x_planes%d" % j, tag="x_planes", align_bytes=64)
+                x_codes[j] = three.tile([P, PASSES, GROUP_ROWS], U32, name="x_codes%d" % j, tag="x_codes", align_bytes=64)
+                x_planes[j] = three.tile([P, PASSES, GROUP_ROWS], U8, name="x_planes%d" % j, tag="x_planes", align_bytes=64)
             rows = slice(pair * PAIR_ROWS, (pair + 1) * PAIR_ROWS)
             for g in range(PASSES):
                 nc.vector.quantize_mx(
@@ -157,8 +173,8 @@ def tile_lstmbaseline_pa_t_kernel(tc, x, w_words, w_scales, b_ih0, b_hh0, out):
             for g in range(PASSES):
                 nc.tensor.matmul_mx(
                     out=acc[:],
-                    lhsT=w_codes[:, g, 2 * c * P : 2 * (c + 1) * P].bitcast(FP4X4),
-                    lhsT_scale=w_planes[:, g, c * P : (c + 1) * P],
+                    lhsT=w_codes[h][:, g, 2 * which * P : 2 * (which + 1) * P].bitcast(FP4X4),
+                    lhsT_scale=w_planes[h][:, g, which * P : (which + 1) * P],
                     rhs=x_codes[j][:, g, :].bitcast(FP8X4),
                     rhs_scale=x_planes[j][:, g, :],
                     start=(g == 0),
@@ -184,7 +200,8 @@ def tile_lstmbaseline_pa_t_kernel(tc, x, w_words, w_scales, b_ih0, b_hh0, out):
             j, h = divmod(v, HALVES)
             if h == 0:
                 hidden[j] = three.tile([P, ROW_BLOCKS, HALVES, BLOCK], F32, name="hidden%d" % j, tag="hidden", align_bytes=64)
-            nc.vector.tensor_tensor(
+            engine = nc.gpsimd if v < ON_GPSIMD else nc.vector
+            engine.tensor_tensor(
                 out=hidden[j][:, :, h, :],
                 in0=gates[v, GATE_O][:].rearrange("p (s a) -> p s a", a=BLOCK),
                 in1=cell_tanh[v][:].rearrange("p (s a) -> p s a", a=BLOCK),
@@ -213,15 +230,24 @@ def tile_lstmbaseline_pa_t_kernel(tc, x, w_words, w_scales, b_ih0, b_hh0, out):
         transpose_x(0)
         quantise_x(0)
         prepare_bias()
-        for v in range(-1, STEPS + 3):
-            when(v + 2, transpose_x)
-            when(v - 3, store)
-            when(v + 2, quantise_x)
-            if v == -1:
-                order_w_columns()
+        transpose_x(1)
+        quantise_x(1)
+        for h in range(HALVES):
+            order_w_columns(h)
+        keep_clock_up(WAIT_FOR_W)
+        following = {0: (2, 3), 1: (4, 5)}
+        turns = {STEPS - 2: (STEPS - 5, STEPS - 4), STEPS - 1: (STEPS - 3,), STEPS: (STEPS - 2, STEPS - 1)}
+        for v in range(STEPS + 1):
             when(v, gate, GATE_I)
             when(v, gate, GATE_G)
             when(v, cell_state)
             when(v - 1, tanh_of_cell)
             when(v, gate, GATE_O)
             when(v - 1, hidden_state)
+            pairs = following.get(v, (v + 4,))
+            for w in pairs:
+                when(w, transpose_x)
+            for piece in turns.get(v, (v - 3,)):
+                when(piece, store)
+            for w in pairs:
+                when(w, quantise_x)

@@ -238,15 +238,16 @@ def tile_lstmbaseline_pa_t_kernel(tc, x, w_words, w_scales, b_ih0, b_hh0, out):
         following = {0: (2, 3), 1: (4, 5)}
         turns = {STEPS - 2: (STEPS - 5, STEPS - 4), STEPS - 1: (STEPS - 3,), STEPS: (STEPS - 2, STEPS - 1)}
         for v in range(STEPS + 1):
+            pairs = following.get(v, (v + 4,))
             when(v, gate, GATE_I)
             when(v, gate, GATE_G)
             when(v, cell_state)
             when(v - 1, tanh_of_cell)
+            for w in pairs[0:-1]:
+                when(w, transpose_x)
             when(v, gate, GATE_O)
             when(v - 1, hidden_state)
-            pairs = following.get(v, (v + 4,))
-            for w in pairs:
-                when(w, transpose_x)
+            when(pairs[-1], transpose_x)
             for piece in turns.get(v, (v - 3,)):
                 when(piece, store)
             for w in pairs:

@@ -29,15 +29,16 @@ HALVES = H // P
 STEPS = GROUPS * HALVES
 assert PAIRS == HALVES
 GATES_IN_W = 4
-COLUMN_TILES = GATES_IN_W * HALVES
 GATE_I, GATE_G, GATE_O = 0, 2, 3
+GATES_USED = (GATE_I, GATE_G, GATE_O)
 BLOCK = 32
 QUADRANTS = P // BLOCK
 ROW_BLOCKS = GROUP_ROWS // BLOCK
 RUN = HALVES * BLOCK
 
-WARM_UP = 5
-WAIT_FOR_W = 4
+WARM_UP = 18
+BETWEEN_PAIRS = 8
+WAIT_FOR_W = 12
 ON_GPSIMD = 12
 
 FLOPS = 2 * B * D * 3 * H
@@ -57,27 +58,23 @@ def tile_lstmbaseline_pa_t_kernel(tc, x, w_words, w_scales, b_ih0, b_hh0, out):
         xt_banks = stack.enter_context(tc.psum_pool(name="xt_banks", bufs=4))
         mx_banks = stack.enter_context(tc.psum_pool(name="mx_banks", bufs=4))
 
-        idle_operand = keep.tile([P, GROUP_ROWS], BF16, name="idle_operand")
+        idle_operand = keep.tile([P, P], BF16, name="idle_operand")
         nc.vector.memset(idle_operand[:], 0.0)
         unread = []
 
         def keep_clock_up(count):
             for n in range(count):
                 unread.append(mx_banks.tile([P, GROUP_ROWS], F32, name="unread%d" % len(unread), tag="acc"))
-                nc.tensor.matmul(out=unread[-1][:], lhsT=idle_operand[:, 0:P], rhs=idle_operand[:], start=True, stop=True)
+                nc.tensor.matmul(out=unread[-1][:, 0:P], lhsT=idle_operand[:], rhs=idle_operand[:], start=True, stop=True)
 
         keep_clock_up(WARM_UP)
 
-        bias_rows = keep.tile([P, P], BF16, name="bias_rows")
-        nc.vector.memset(bias_rows[:], 0.0)
-        for first_row, vector in ((0, b_ih0), (COLUMN_TILES, b_hh0)):
-            for h in range(HALVES):
-                nc.scalar.dma_start(
-                    out=bias_rows[first_row + h : first_row + COLUMN_TILES : HALVES, :].rearrange(
-                        "G (i b) -> G i b", b=BLOCK
-                    ),
-                    in_=vector.rearrange("(G i h b) -> h G i b", i=QUADRANTS, h=HALVES, b=BLOCK)[h],
-                )
+        bias_rows = keep.tile([P, H], BF16, name="bias_rows")
+        nc.gpsimd.memset(bias_rows[:], 0.0)
+        for first_row, vector in ((0, b_ih0), (GATES_IN_W, b_hh0)):
+            nc.scalar.dma_start(
+                out=bias_rows[first_row : first_row + GATES_IN_W, :], in_=vector.rearrange("(G n) -> G n", n=H)
+            )
 
         x_sb = []
         for w in range(GROUPS * PAIRS):
@@ -95,8 +92,15 @@ def tile_lstmbaseline_pa_t_kernel(tc, x, w_words, w_scales, b_ih0, b_hh0, out):
                 out=w_planes_in[32 * quadrant : 32 * quadrant + 4, :, :].bitcast(I32),
                 in_=w_scales[:, 4 * quadrant : 4 * quadrant + 4, :].rearrange("g r n -> r g n").bitcast(I32),
             )
-        w_codes_in = keep.tile([P, PASSES, 2 * GATES_IN_W * H], U8, name="w_codes_in", align_bytes=64)
-        nc.sync.dma_start(out=w_codes_in[:].bitcast(I32), in_=w_words.rearrange("g p n -> p g n").bitcast(I32))
+        w_codes_in = keep.tile([P, PASSES, 2 * len(GATES_USED) * H], U8, name="w_codes_in", align_bytes=64)
+        words_of_gates = w_words.rearrange("g p n -> p g n")
+        nc.sync.dma_start(
+            out=w_codes_in[:, :, 0 : 2 * H].bitcast(I32),
+            in_=words_of_gates[:, :, 2 * GATE_I * H : 2 * (GATE_I + 1) * H].bitcast(I32),
+        )
+        nc.sync.dma_start(
+            out=w_codes_in[:, :, 2 * H :].bitcast(I32), in_=words_of_gates[:, :, 2 * GATE_G * H :].bitcast(I32)
+        )
         for w in range(PAIRS, GROUPS * PAIRS):
             load_x(w)
 
@@ -109,29 +113,47 @@ def tile_lstmbaseline_pa_t_kernel(tc, x, w_words, w_scales, b_ih0, b_hh0, out):
         nc.vector.memset(warm[:], 0.0)
         nc.scalar.activation(out=warm[:], in_=warm[:], func=ACT.Sigmoid)
 
-        w_codes, w_planes = [], []
+        w_codes, w_planes = {}, []
         for h in range(HALVES):
-            w_codes.append(keep.tile([P, PASSES, 2 * GATES_IN_W * P], U8, name="w_codes%d" % h, align_bytes=64))
             w_planes.append(keep.tile([P, PASSES, GATES_IN_W * P], U8, name="w_planes%d" % h, align_bytes=64))
+            for which in GATES_USED:
+                w_codes[h, which] = keep.tile([P, PASSES, 2 * P], U8, name="w_codes%d_%d" % (h, which), align_bytes=64)
 
-        def order_w_columns(h):
-            for ordered, arrived in ((w_planes[h], w_planes_in), (w_codes[h], w_codes_in)):
-                nc.vector.tensor_copy(
-                    out=ordered[:].bitcast(I32).rearrange("p g (G i w) -> p (g G) i w", G=GATES_IN_W, i=QUADRANTS),
-                    in_=arrived[:].bitcast(I32).rearrange(
-                        "p g (G i h w) -> p (g G) i h w", G=GATES_IN_W, h=HALVES, i=QUADRANTS
-                    )[:, :, :, h, :],
-                )
+        def order_w_planes(h):
+            nc.vector.tensor_copy(
+                out=w_planes[h][:].bitcast(I32).rearrange("p g (G i w) -> p (g G) i w", G=GATES_IN_W, i=QUADRANTS),
+                in_=w_planes_in[:].bitcast(I32).rearrange(
+                    "p g (G i h w) -> p (g G) i h w", G=GATES_IN_W, h=HALVES, i=QUADRANTS
+                )[:, :, :, h, :],
+            )
 
-        bias = keep.tile([P, COLUMN_TILES], F32, name="bias")
+        def order_w_codes(h, which):
+            at = 2 * H * GATES_USED.index(which)
+            nc.vector.tensor_copy(
+                out=w_codes[h, which][:].bitcast(I32).rearrange("p g (i w) -> p g i w", i=QUADRANTS),
+                in_=w_codes_in[:, :, at : at + 2 * H].bitcast(I32).rearrange(
+                    "p g (i h w) -> p g i h w", h=HALVES, i=QUADRANTS
+                )[:, :, :, h, :],
+            )
 
-        def prepare_bias():
-            bias_ps = xt_banks.tile([P, P], BF16, name="bias_ps", tag="xt")
-            nc.tensor.transpose(bias_ps[:], bias_rows[:], ident_bf16[:])
-            bias_parts = keep.tile([P, 2 * COLUMN_TILES], F32, name="bias_parts")
-            nc.vector.tensor_copy(out=bias_parts[:], in_=bias_ps[:, 0 : 2 * COLUMN_TILES])
+        bias = keep.tile([P, HALVES, GATES_IN_W], F32, name="bias")
+
+        bias_ordered = keep.tile([P, HALVES, P], BF16, name="bias_ordered")
+        nc.gpsimd.tensor_copy(
+            out=bias_ordered[:].rearrange("p h (i b) -> p h i b", b=BLOCK),
+            in_=bias_rows[:].rearrange("p (i h b) -> p h i b", h=HALVES, b=BLOCK),
+        )
+        def transpose_bias():
+            bias_ps = xt_banks.tile([P, HALVES, P], BF16, name="bias_ps", tag="xt")
+            for h in range(HALVES):
+                nc.tensor.transpose(bias_ps[:, h, :], bias_ordered[:, h, :], ident_bf16[:])
+            return bias_ps
+
+        def add_biases(bias_ps):
+            bias_parts = keep.tile([P, HALVES, 2 * GATES_IN_W], F32, name="bias_parts")
+            nc.vector.tensor_copy(out=bias_parts[:], in_=bias_ps[:, :, 0 : 2 * GATES_IN_W])
             nc.vector.tensor_tensor(
-                out=bias[:], in0=bias_parts[:, 0:COLUMN_TILES], in1=bias_parts[:, COLUMN_TILES:], op=ALU.add
+                out=bias[:], in0=bias_parts[:, :, 0:GATES_IN_W], in1=bias_parts[:, :, GATES_IN_W:], op=ALU.add
             )
 
         grouped, x_codes, x_planes = {}, {}, {}
@@ -148,10 +170,8 @@ def tile_lstmbaseline_pa_t_kernel(tc, x, w_words, w_scales, b_ih0, b_hh0, out):
                             x_sb[w][:, i, :].bitcast(F32)[:, g * WORDS + u : (g + 1) * WORDS : 2],
                             ident_f32[:],
                         )
-                copy_out = nc.scalar.copy if (w < PAIRS or (g == 1 and w % 2 == 0)) else nc.vector.tensor_copy
+                copy_out = nc.scalar.copy if g == 1 and (w < PAIRS or w % 2 == 0) else nc.vector.tensor_copy
                 copy_out(out=grouped[w][:, g, :, :].bitcast(F32), in_=bank[:].rearrange("p u r -> p r u"))
-                if w < PAIRS:
-                    keep_clock_up(1)
 
         def quantise_x(w):
             j, pair = divmod(w, PAIRS)
@@ -168,12 +188,11 @@ def tile_lstmbaseline_pa_t_kernel(tc, x, w_words, w_scales, b_ih0, b_hh0, out):
 
         def gate(v, which):
             j, h = divmod(v, HALVES)
-            c = which * HALVES + h
             acc = mx_banks.tile([P, GROUP_ROWS], F32, name="acc%d_%d" % (v, which), tag="acc")
             for g in range(PASSES):
                 nc.tensor.matmul_mx(
                     out=acc[:],
-                    lhsT=w_codes[h][:, g, 2 * which * P : 2 * (which + 1) * P].bitcast(FP4X4),
+                    lhsT=w_codes[h, which][:, g, :].bitcast(FP4X4),
                     lhsT_scale=w_planes[h][:, g, which * P : (which + 1) * P],
                     rhs=x_codes[j][:, g, :].bitcast(FP8X4),
                     rhs_scale=x_planes[j][:, g, :],
@@ -185,7 +204,7 @@ def tile_lstmbaseline_pa_t_kernel(tc, x, w_words, w_scales, b_ih0, b_hh0, out):
                 out=gates[v, which][:],
                 in_=acc[:],
                 func=ACT.Tanh if which == GATE_G else ACT.Sigmoid,
-                bias=bias[:, c : c + 1],
+                bias=bias[:, h, which : which + 1],
             )
 
         def cell_state(v):
@@ -229,12 +248,19 @@ def tile_lstmbaseline_pa_t_kernel(tc, x, w_words, w_scales, b_ih0, b_hh0, out):
 
         transpose_x(0)
         quantise_x(0)
-        prepare_bias()
+        keep_clock_up(BETWEEN_PAIRS)
         transpose_x(1)
+        bias_ps = transpose_bias()
+        order_w_planes(0)
+        order_w_codes(0, GATE_I)
         quantise_x(1)
-        for h in range(HALVES):
-            order_w_columns(h)
         keep_clock_up(WAIT_FOR_W)
+        add_biases(bias_ps)
+        order_w_codes(0, GATE_G)
+        order_w_codes(0, GATE_O)
+        order_w_planes(1)
+        for which in GATES_USED:
+            order_w_codes(1, which)
         following = {0: (2, 3), 1: (4, 5)}
         turns = {STEPS - 2: (STEPS - 5, STEPS - 4), STEPS - 1: (STEPS - 3,), STEPS: (STEPS - 2, STEPS - 1)}
         for v in range(STEPS + 1):

@@ -170,7 +170,7 @@ def tile_lstmbaseline_pa_t_kernel(tc, x, w_words, w_scales, b_ih0, b_hh0, out):
                             x_sb[w][:, i, :].bitcast(F32)[:, g * WORDS + u : (g + 1) * WORDS : 2],
                             ident_f32[:],
                         )
-                copy_out = nc.scalar.copy if g == 1 and (w < PAIRS or w % 2 == 0) else nc.vector.tensor_copy
+                copy_out = nc.scalar.copy if g == 1 and w % 4 != 3 else nc.vector.tensor_copy
                 copy_out(out=grouped[w][:, g, :, :].bitcast(F32), in_=bank[:].rearrange("p u r -> p r u"))
 
         def quantise_x(w):

@@ -38,7 +38,7 @@ RUN = HALVES * BLOCK
 
 WARM_UP = 18
 BETWEEN_PAIRS = 8
-WAIT_FOR_W = 12
+WAIT_FOR_W = 6
 ON_GPSIMD = 12
 
 FLOPS = 2 * B * D * 3 * H
@@ -55,6 +55,7 @@ def tile_lstmbaseline_pa_t_kernel(tc, x, w_words, w_scales, b_ih0, b_hh0, out):
         keep = stack.enter_context(tc.tile_pool(name="keep", bufs=1))
         two = stack.enter_context(tc.tile_pool(name="two", bufs=2))
         three = stack.enter_context(tc.tile_pool(name="three", bufs=3))
+        five = stack.enter_context(tc.tile_pool(name="five", bufs=5))
         xt_banks = stack.enter_context(tc.psum_pool(name="xt_banks", bufs=4))
         mx_banks = stack.enter_context(tc.psum_pool(name="mx_banks", bufs=4))
 
@@ -170,7 +171,7 @@ def tile_lstmbaseline_pa_t_kernel(tc, x, w_words, w_scales, b_ih0, b_hh0, out):
                             x_sb[w][:, i, :].bitcast(F32)[:, g * WORDS + u : (g + 1) * WORDS : 2],
                             ident_f32[:],
                         )
-                copy_out = nc.scalar.copy if g == 1 and w % 4 != 3 else nc.vector.tensor_copy
+                copy_out = nc.scalar.copy if g == 1 and (w < PAIRS or w % 4 != 1) else nc.vector.tensor_copy
                 copy_out(out=grouped[w][:, g, :, :].bitcast(F32), in_=bank[:].rearrange("p u r -> p r u"))
 
         def quantise_x(w):
@@ -186,44 +187,58 @@ def tile_lstmbaseline_pa_t_kernel(tc, x, w_words, w_scales, b_ih0, b_hh0, out):
                     in_=grouped[w][:, g, :, :].rearrange("p r t -> p (r t)"),
                 )
 
-        def gate(v, which):
+        def part_of_rows(part):
+            return slice(0, GROUP_ROWS) if part is None else slice(part * PAIR_ROWS, (part + 1) * PAIR_ROWS)
+
+        def gate(v, which, part=None):
             j, h = divmod(v, HALVES)
-            acc = mx_banks.tile([P, GROUP_ROWS], F32, name="acc%d_%d" % (v, which), tag="acc")
-            for g in range(PASSES):
-                nc.tensor.matmul_mx(
-                    out=acc[:],
-                    lhsT=w_codes[h, which][:, g, :].bitcast(FP4X4),
-                    lhsT_scale=w_planes[h][:, g, which * P : (which + 1) * P],
-                    rhs=x_codes[j][:, g, :].bitcast(FP8X4),
-                    rhs_scale=x_planes[j][:, g, :],
-                    start=(g == 0),
-                    stop=(g == PASSES - 1),
-                )
-            gates[v, which] = two.tile([P, GROUP_ROWS], F32, name="gate%d_%d" % (which, v), tag="gate%d" % which)
+            rows = part_of_rows(part)
+            chunk = GROUP_ROWS if part is None else P
+            acc = mx_banks.tile([P, GROUP_ROWS], F32, name="acc%d_%d_%d" % (v, which, rows.start), tag="acc")
+            for start in range(rows.start, rows.stop, chunk):
+                for g in range(PASSES):
+                    nc.tensor.matmul_mx(
+                        out=acc[:, start - rows.start : start - rows.start + chunk],
+                        lhsT=w_codes[h, which][:, g, :].bitcast(FP4X4),
+                        lhsT_scale=w_planes[h][:, g, which * P : (which + 1) * P],
+                        rhs=x_codes[j][:, g, start : start + chunk].bitcast(FP8X4),
+                        rhs_scale=x_planes[j][:, g, start : start + chunk],
+                        start=(g == 0),
+                        stop=(g == PASSES - 1),
+                    )
+            if (v, which) not in gates:
+                gates[v, which] = two.tile([P, GROUP_ROWS], F32, name="gate%d_%d" % (which, v), tag="gate%d" % which)
             nc.scalar.activation(
-                out=gates[v, which][:],
-                in_=acc[:],
+                out=gates[v, which][:, rows],
+                in_=acc[:, 0 : rows.stop - rows.start],
                 func=ACT.Tanh if which == GATE_G else ACT.Sigmoid,
                 bias=bias[:, h, which : which + 1],
             )
 
-        def cell_state(v):
-            cell[v] = two.tile([P, GROUP_ROWS], F32, name="cell%d" % v, tag="cell")
-            nc.vector.tensor_tensor(out=cell[v][:], in0=gates[v, GATE_I][:], in1=gates[v, GATE_G][:], op=ALU.mult)
+        def cell_state(v, part=None):
+            rows = part_of_rows(part)
+            if v not in cell:
+                cell[v] = two.tile([P, GROUP_ROWS], F32, name="cell%d" % v, tag="cell")
+            nc.vector.tensor_tensor(
+                out=cell[v][:, rows], in0=gates[v, GATE_I][:, rows], in1=gates[v, GATE_G][:, rows], op=ALU.mult
+            )
 
-        def tanh_of_cell(v):
-            cell_tanh[v] = two.tile([P, GROUP_ROWS], F32, name="cell_tanh%d" % v, tag="cell_tanh")
-            nc.scalar.activation(out=cell_tanh[v][:], in_=cell[v][:], func=ACT.Tanh)
+        def tanh_of_cell(v, part=None):
+            rows = part_of_rows(part)
+            if v not in cell_tanh:
+                cell_tanh[v] = two.tile([P, GROUP_ROWS], F32, name="cell_tanh%d" % v, tag="cell_tanh")
+            nc.scalar.activation(out=cell_tanh[v][:, rows], in_=cell[v][:, rows], func=ACT.Tanh)
 
-        def hidden_state(v):
+        def hidden_state(v, part=None):
             j, h = divmod(v, HALVES)
-            if h == 0:
+            rows = part_of_rows(part)
+            if j not in hidden:
                 hidden[j] = three.tile([P, ROW_BLOCKS, HALVES, BLOCK], F32, name="hidden%d" % j, tag="hidden", align_bytes=64)
             engine = nc.gpsimd if v < ON_GPSIMD else nc.vector
             engine.tensor_tensor(
-                out=hidden[j][:, :, h, :],
-                in0=gates[v, GATE_O][:].rearrange("p (s a) -> p s a", a=BLOCK),
-                in1=cell_tanh[v][:].rearrange("p (s a) -> p s a", a=BLOCK),
+                out=hidden[j][:, rows.start // BLOCK : rows.stop // BLOCK, h, :],
+                in0=gates[v, GATE_O][:, rows].rearrange("p (s a) -> p s a", a=BLOCK),
+                in1=cell_tanh[v][:, rows].rearrange("p (s a) -> p s a", a=BLOCK),
                 op=ALU.mult,
             )
 
@@ -231,7 +246,7 @@ def tile_lstmbaseline_pa_t_kernel(tc, x, w_words, w_scales, b_ih0, b_hh0, out):
             j, part = divmod(piece, 2)
             blocks = ROW_BLOCKS // 2
             width = blocks * RUN
-            turned[piece] = three.tile([P, width], F32, name="turned%d" % piece, tag="turned", align_bytes=64)
+            turned[piece] = five.tile([P, width], F32, name="turned%d" % piece, tag="turned", align_bytes=64)
             nc.vector.transpose(
                 out=turned[piece][:],
                 in_=hidden[j][:].rearrange("p s h a -> p (s h a)")[:, part * width : (part + 1) * width],
@@ -252,29 +267,48 @@ def tile_lstmbaseline_pa_t_kernel(tc, x, w_words, w_scales, b_ih0, b_hh0, out):
         transpose_x(1)
         bias_ps = transpose_bias()
         order_w_planes(0)
-        order_w_codes(0, GATE_I)
+        for which in GATES_USED:
+            order_w_codes(0, which)
+        add_biases(bias_ps)
         quantise_x(1)
         keep_clock_up(WAIT_FOR_W)
-        add_biases(bias_ps)
-        order_w_codes(0, GATE_G)
-        order_w_codes(0, GATE_O)
-        order_w_planes(1)
-        for which in GATES_USED:
-            order_w_codes(1, which)
-        following = {0: (2, 3), 1: (4, 5)}
-        turns = {STEPS - 2: (STEPS - 5, STEPS - 4), STEPS - 1: (STEPS - 3,), STEPS: (STEPS - 2, STEPS - 1)}
-        for v in range(STEPS + 1):
-            pairs = following.get(v, (v + 4,))
-            when(v, gate, GATE_I)
-            when(v, gate, GATE_G)
-            when(v, cell_state)
-            when(v - 1, tanh_of_cell)
-            for w in pairs[0:-1]:
-                when(w, transpose_x)
-            when(v, gate, GATE_O)
-            when(v - 1, hidden_state)
-            when(pairs[-1], transpose_x)
+        for part in range(PAIRS):
+            gate(0, GATE_I, part)
+            gate(0, GATE_G, part)
+            cell_state(0, part)
+            if part == 0:
+                gate(0, GATE_O, part)
+                order_w_planes(1)
+                for which in GATES_USED:
+                    order_w_codes(1, which)
+        transpose_x(2)
+        gate(0, GATE_O, PAIRS - 1)
+        transpose_x(3)
+        quantise_x(2)
+        quantise_x(3)
+        turns = {STEPS - 3: (STEPS - 6, STEPS - 5), STEPS - 2: (STEPS - 4, STEPS - 3)}
+        for v in range(1, STEPS - 1):
+            gate(v, GATE_I)
+            gate(v, GATE_G)
+            cell_state(v)
+            tanh_of_cell(v - 1)
+            gate(v, GATE_O)
+            hidden_state(v - 1)
+            when(v + 3, transpose_x)
             for piece in turns.get(v, (v - 3,)):
                 when(piece, store)
-            for w in pairs:
-                when(w, quantise_x)
+            when(v + 3, quantise_x)
+        last = STEPS - 1
+        gate(last, GATE_I, 0)
+        gate(last, GATE_G, 0)
+        cell_state(last, 0)
+        tanh_of_cell(last - 1)
+        gate(last, GATE_I, 1)
+        gate(last, GATE_G, 1)
+        hidden_state(last - 1)
+        cell_state(last, 1)
+        for part in range(2):
+            gate(last, GATE_O, part)
+            tanh_of_cell(last, part)
+            hidden_state(last, part)
+            store(last - 1 + part)

@@ -38,7 +38,7 @@ RUN = HALVES * BLOCK
 
 WARM_UP = 18
 BETWEEN_PAIRS = 8
-WAIT_FOR_W = 6
+WAIT_FOR_W = 12
 ON_GPSIMD = 12
 
 FLOPS = 2 * B * D * 3 * H
@@ -171,7 +171,7 @@ def tile_lstmbaseline_pa_t_kernel(tc, x, w_words, w_scales, b_ih0, b_hh0, out):
                             x_sb[w][:, i, :].bitcast(F32)[:, g * WORDS + u : (g + 1) * WORDS : 2],
                             ident_f32[:],
                         )
-                copy_out = nc.scalar.copy if g == 1 and (w < PAIRS or w % 4 != 1) else nc.vector.tensor_copy
+                copy_out = nc.scalar.copy if g == 1 and (w < PAIRS or w % 2 == 0) else nc.vector.tensor_copy
                 copy_out(out=grouped[w][:, g, :, :].bitcast(F32), in_=bank[:].rearrange("p u r -> p r u"))
 
         def quantise_x(w):
@@ -288,16 +288,20 @@ def tile_lstmbaseline_pa_t_kernel(tc, x, w_words, w_scales, b_ih0, b_hh0, out):
         quantise_x(3)
         turns = {STEPS - 3: (STEPS - 6, STEPS - 5), STEPS - 2: (STEPS - 4, STEPS - 3)}
         for v in range(1, STEPS - 1):
+            pairs = (4, 5) if v == 1 else (v + 4,)
             gate(v, GATE_I)
             gate(v, GATE_G)
             cell_state(v)
             tanh_of_cell(v - 1)
+            for w in pairs[0:-1]:
+                transpose_x(w)
             gate(v, GATE_O)
             hidden_state(v - 1)
-            when(v + 3, transpose_x)
+            when(pairs[-1], transpose_x)
             for piece in turns.get(v, (v - 3,)):
                 when(piece, store)
-            when(v + 3, quantise_x)
+            for w in pairs:
+                when(w, quantise_x)
         last = STEPS - 1
         gate(last, GATE_I, 0)
         gate(last, GATE_G, 0)

from contextlib import ExitStack

import concourse.mybir as mybir
from concourse.masks import make_identity

F32 = mybir.dt.float32
BF16 = mybir.dt.bfloat16
I32 = mybir.dt.int32
U32 = mybir.dt.uint32
U8 = mybir.dt.uint8
FP8X4 = mybir.dt.float8_e4m3fn_x4
FP4X4 = mybir.dt.float4_e2m1fn_x4
ACT = mybir.ActivationFunctionType
ALU = mybir.AluOpType

B, D, H = 4096, 1024, 256
P = 128
PACK = 4
K_PASS = P * PACK
PASSES = D // K_PASS
WORDS = K_PASS // 2
ROW_TILES = B // P
GROUP_ROWS = 512
GROUP_TILES = GROUP_ROWS // P
GROUPS = B // GROUP_ROWS
PAIR_ROWS = 2 * P
PAIRS = GROUP_ROWS // PAIR_ROWS
HALVES = H // P
STEPS = GROUPS * HALVES
assert PAIRS == HALVES
GATES_IN_W = 4
GATE_I, GATE_G, GATE_O = 0, 2, 3
GATES_USED = (GATE_I, GATE_G, GATE_O)
BLOCK = 32
QUADRANTS = P // BLOCK
ROW_BLOCKS = GROUP_ROWS // BLOCK
RUN = HALVES * BLOCK

WARM_UP = 18
BETWEEN_PAIRS = 8
WAIT_FOR_W = 12
ON_GPSIMD = 12

FLOPS = 2 * B * D * 3 * H
BYTES = B * D * 2 + B * H * 4 + 3 * H * D // 2 + 3 * H * D // 32 + 2 * 3 * H * 2


def tile_lstmbaseline_pa_t_kernel(tc, x, w_words, w_scales, b_ih0, b_hh0, out):
    nc = tc.nc
    x_rows = x.rearrange("(t p) k -> p t k", p=P)
    out_runs = out.rearrange("(j s a) (i e) -> j i a s e", s=ROW_BLOCKS, a=BLOCK, e=RUN)

    with ExitStack() as stack:
        stack.enter_context(tc.manual_schedule())
        keep = stack.enter_context(tc.tile_pool(name="keep", bufs=1))
        two = stack.enter_context(tc.tile_pool(name="two", bufs=2))
        three = stack.enter_context(tc.tile_pool(name="three", bufs=3))
        five = stack.enter_context(tc.tile_pool(name="five", bufs=5))
        xt_banks = stack.enter_context(tc.psum_pool(name="xt_banks", bufs=4))
        mx_banks = stack.enter_context(tc.psum_pool(name="mx_banks", bufs=4))

        idle_operand = keep.tile([P, P], BF16, name="idle_operand")
        nc.vector.memset(idle_operand[:], 0.0)
        unread = []

        def keep_clock_up(count):
            for n in range(count):
                unread.append(mx_banks.tile([P, GROUP_ROWS], F32, name="unread%d" % len(unread), tag="acc"))
                nc.tensor.matmul(out=unread[-1][:, 0:P], lhsT=idle_operand[:], rhs=idle_operand[:], start=True, stop=True)

        keep_clock_up(WARM_UP)

        bias_rows = keep.tile([P, H], BF16, name="bias_rows")
        nc.gpsimd.memset(bias_rows[:], 0.0)
        for first_row, vector in ((0, b_ih0), (GATES_IN_W, b_hh0)):
            nc.scalar.dma_start(
                out=bias_rows[first_row : first_row + GATES_IN_W, :], in_=vector.rearrange("(G n) -> G n", n=H)
            )

        x_sb = []
        for w in range(GROUPS * PAIRS):
            x_sb.append(keep.tile([P, 2, D], BF16, name="x%d" % w))

        def load_x(w):
            nc.sync.dma_start(out=x_sb[w][:], in_=x_rows[:, 2 * w : 2 * (w + 1), :])

        for w in range(PAIRS):
            load_x(w)
        w_planes_in = keep.tile([P, PASSES, GATES_IN_W * H], U8, name="w_planes_in", align_bytes=64)
        nc.vector.memset(w_planes_in[:].bitcast(I32), 0)
        for quadrant in range(4):
            nc.sync.dma_start(
                out=w_planes_in[32 * quadrant : 32 * quadrant + 4, :, :].bitcast(I32),
                in_=w_scales[:, 4 * quadrant : 4 * quadrant + 4, :].rearrange("g r n -> r g n").bitcast(I32),
            )
        w_codes_in = keep.tile([P, PASSES, 2 * len(GATES_USED) * H], U8, name="w_codes_in", align_bytes=64)
        words_of_gates = w_words.rearrange("g p n -> p g n")
        nc.sync.dma_start(
            out=w_codes_in[:, :, 0 : 2 * H].bitcast(I32),
            in_=words_of_gates[:, :, 2 * GATE_I * H : 2 * (GATE_I + 1) * H].bitcast(I32),
        )
        nc.sync.dma_start(
            out=w_codes_in[:, :, 2 * H :].bitcast(I32), in_=words_of_gates[:, :, 2 * GATE_G * H :].bitcast(I32)
        )
        for w in range(PAIRS, GROUPS * PAIRS):
            load_x(w)

        ident_f32 = keep.tile([P, P], F32, name="ident_f32")
        make_identity(nc, ident_f32[:])
        ident_bf16 = keep.tile([P, P], BF16, name="ident_bf16")
        nc.vector.tensor_copy(out=ident_bf16[:], in_=ident_f32[:])

        warm = keep.tile([P, 1], F32, name="warm")
        nc.vector.memset(warm[:], 0.0)
        nc.scalar.activation(out=warm[:], in_=warm[:], func=ACT.Sigmoid)

        w_codes, w_planes = {}, []
        for h in range(HALVES):
            w_planes.append(keep.tile([P, PASSES, GATES_IN_W * P], U8, name="w_planes%d" % h, align_bytes=64))
            for which in GATES_USED:
                w_codes[h, which] = keep.tile([P, PASSES, 2 * P], U8, name="w_codes%d_%d" % (h, which), align_bytes=64)

        def order_w_planes(h):
            nc.vector.tensor_copy(
                out=w_planes[h][:].bitcast(I32).rearrange("p g (G i w) -> p (g G) i w", G=GATES_IN_W, i=QUADRANTS),
                in_=w_planes_in[:].bitcast(I32).rearrange(
                    "p g (G i h w) -> p (g G) i h w", G=GATES_IN_W, h=HALVES, i=QUADRANTS
                )[:, :, :, h, :],
            )

        def order_w_codes(h, which):
            at = 2 * H * GATES_USED.index(which)
            nc.vector.tensor_copy(
                out=w_codes[h, which][:].bitcast(I32).rearrange("p g (i w) -> p g i w", i=QUADRANTS),
                in_=w_codes_in[:, :, at : at + 2 * H].bitcast(I32).rearrange(
                    "p g (i h w) -> p g i h w", h=HALVES, i=QUADRANTS
                )[:, :, :, h, :],
            )

        bias = keep.tile([P, HALVES, GATES_IN_W], F32, name="bias")

        bias_ordered = keep.tile([P, HALVES, P], BF16, name="bias_ordered")
        nc.gpsimd.tensor_copy(
            out=bias_ordered[:].rearrange("p h (i b) -> p h i b", b=BLOCK),
            in_=bias_rows[:].rearrange("p (i h b) -> p h i b", h=HALVES, b=BLOCK),
        )
        def transpose_bias():
            bias_ps = xt_banks.tile([P, HALVES, P], BF16, name="bias_ps", tag="xt")
            for h in range(HALVES):
                nc.tensor.transpose(bias_ps[:, h, :], bias_ordered[:, h, :], ident_bf16[:])
            return bias_ps

        def add_biases(bias_ps):
            bias_parts = keep.tile([P, HALVES, 2 * GATES_IN_W], F32, name="bias_parts")
            nc.vector.tensor_copy(out=bias_parts[:], in_=bias_ps[:, :, 0 : 2 * GATES_IN_W])
            nc.vector.tensor_tensor(
                out=bias[:], in0=bias_parts[:, :, 0:GATES_IN_W], in1=bias_parts[:, :, GATES_IN_W:], op=ALU.add
            )

        grouped, x_codes, x_planes = {}, {}, {}
        gates, cell, cell_tanh, hidden, turned = {}, {}, {}, {}, {}

        def transpose_x(w):
            grouped[w] = three.tile([P, PASSES, PAIR_ROWS, PACK], BF16, name="grouped%d" % w, tag="grouped", align_bytes=64)
            for g in range(PASSES):
                bank = xt_banks.tile([P, 2, PAIR_ROWS], F32, name="xt%d_%d" % (w, g), tag="xt")
                for u in range(2):
                    for i in range(2):
                        nc.tensor.transpose(
                            bank[:, u, i * P : (i + 1) * P],
                            x_sb[w][:, i, :].bitcast(F32)[:, g * WORDS + u : (g + 1) * WORDS : 2],
                            ident_f32[:],
                        )
                copy_out = nc.scalar.copy if g == 1 and (w < PAIRS or w % 2 == 0) else nc.vector.tensor_copy
                copy_out(out=grouped[w][:, g, :, :].bitcast(F32), in_=bank[:].rearrange("p u r -> p r u"))

        def quantise_x(w):
            j, pair = divmod(w, PAIRS)
            if pair == 0:
                x_codes[j] = three.tile([P, PASSES, GROUP_ROWS], U32, name="x_codes%d" % j, tag="x_codes", align_bytes=64)
                x_planes[j] = three.tile([P, PASSES, GROUP_ROWS], U8, name="x_planes%d" % j, tag="x_planes", align_bytes=64)
            rows = slice(pair * PAIR_ROWS, (pair + 1) * PAIR_ROWS)
            for g in range(PASSES):
                nc.vector.quantize_mx(
                    out=x_codes[j][:, g, rows].bitcast(FP8X4),
                    scales=x_planes[j][:, g, rows],
                    in_=grouped[w][:, g, :, :].rearrange("p r t -> p (r t)"),
                )

        def part_of_rows(part):
            return slice(0, GROUP_ROWS) if part is None else slice(part * PAIR_ROWS, (part + 1) * PAIR_ROWS)

        def gate(v, which, part=None):
            j, h = divmod(v, HALVES)
            rows = part_of_rows(part)
            chunk = GROUP_ROWS if part is None else P
            acc = mx_banks.tile([P, GROUP_ROWS], F32, name="acc%d_%d_%d" % (v, which, rows.start), tag="acc")
            for start in range(rows.start, rows.stop, chunk):
                for g in range(PASSES):
                    nc.tensor.matmul_mx(
                        out=acc[:, start - rows.start : start - rows.start + chunk],
                        lhsT=w_codes[h, which][:, g, :].bitcast(FP4X4),
                        lhsT_scale=w_planes[h][:, g, which * P : (which + 1) * P],
                        rhs=x_codes[j][:, g, start : start + chunk].bitcast(FP8X4),
                        rhs_scale=x_planes[j][:, g, start : start + chunk],
                        start=(g == 0),
                        stop=(g == PASSES - 1),
                    )
            if (v, which) not in gates:
                gates[v, which] = two.tile([P, GROUP_ROWS], F32, name="gate%d_%d" % (which, v), tag="gate%d" % which)
            nc.scalar.activation(
                out=gates[v, which][:, rows],
                in_=acc[:, 0 : rows.stop - rows.start],
                func=ACT.Tanh if which == GATE_G else ACT.Sigmoid,
                bias=bias[:, h, which : which + 1],
            )

        def cell_state(v, part=None):
            rows = part_of_rows(part)
            if v not in cell:
                cell[v] = two.tile([P, GROUP_ROWS], F32, name="cell%d" % v, tag="cell")
            nc.vector.tensor_tensor(
                out=cell[v][:, rows], in0=gates[v, GATE_I][:, rows], in1=gates[v, GATE_G][:, rows], op=ALU.mult
            )

        def tanh_of_cell(v, part=None):
            rows = part_of_rows(part)
            if v not in cell_tanh:
                cell_tanh[v] = two.tile([P, GROUP_ROWS], F32, name="cell_tanh%d" % v, tag="cell_tanh")
            nc.scalar.activation(out=cell_tanh[v][:, rows], in_=cell[v][:, rows], func=ACT.Tanh)

        def hidden_state(v, part=None):
            j, h = divmod(v, HALVES)
            rows = part_of_rows(part)
            if j not in hidden:
                hidden[j] = three.tile([P, ROW_BLOCKS, HALVES, BLOCK], F32, name="hidden%d" % j, tag="hidden", align_bytes=64)
            engine = nc.gpsimd if v < ON_GPSIMD else nc.vector
            engine.tensor_tensor(
                out=hidden[j][:, rows.start // BLOCK : rows.stop // BLOCK, h, :],
                in0=gates[v, GATE_O][:, rows].rearrange("p (s a) -> p s a", a=BLOCK),
                in1=cell_tanh[v][:, rows].rearrange("p (s a) -> p s a", a=BLOCK),
                op=ALU.mult,
            )

        def store(piece):
            j, part = divmod(piece, 2)
            blocks = ROW_BLOCKS // 2
            width = blocks * RUN
            turned[piece] = five.tile([P, width], F32, name="turned%d" % piece, tag="turned", align_bytes=64)
            nc.vector.transpose(
                out=turned[piece][:],
                in_=hidden[j][:].rearrange("p s h a -> p (s h a)")[:, part * width : (part + 1) * width],
            )
            for i in range(QUADRANTS):
                nc.sync.dma_start(
                    out=out_runs[j, i, :, part * blocks : (part + 1) * blocks, :],
                    in_=turned[piece][i * BLOCK : (i + 1) * BLOCK, :].rearrange("a (s e) -> a s e", e=RUN),
                )

        def when(index, stage, *args):
            if 0 <= index < STEPS:
                stage(index, *args)

        transpose_x(0)
        quantise_x(0)
        keep_clock_up(BETWEEN_PAIRS)
        transpose_x(1)
        bias_ps = transpose_bias()
        order_w_planes(0)
        for which in GATES_USED:
            order_w_codes(0, which)
        add_biases(bias_ps)
        quantise_x(1)
        keep_clock_up(WAIT_FOR_W)
        for part in range(PAIRS):
            gate(0, GATE_I, part)
            gate(0, GATE_G, part)
            cell_state(0, part)
            if part == 0:
                gate(0, GATE_O, part)
                order_w_planes(1)
                for which in GATES_USED:
                    order_w_codes(1, which)
        transpose_x(2)
        gate(0, GATE_O, PAIRS - 1)
        transpose_x(3)
        quantise_x(2)
        quantise_x(3)
        turns = {STEPS - 3: (STEPS - 6, STEPS - 5), STEPS - 2: (STEPS - 4, STEPS - 3)}
        for v in range(1, STEPS - 1):
            pairs = (4, 5) if v == 1 else (v + 4,)
            gate(v, GATE_I)
            gate(v, GATE_G)
            cell_state(v)
            tanh_of_cell(v - 1)
            for w in pairs[0:-1]:
                transpose_x(w)
            gate(v, GATE_O)
            hidden_state(v - 1)
            when(pairs[-1], transpose_x)
            for piece in turns.get(v, (v - 3,)):
                when(piece, store)
            for w in pairs:
                when(w, quantise_x)
        last = STEPS - 1
        gate(last, GATE_I, 0)
        gate(last, GATE_G, 0)
        cell_state(last, 0)
        tanh_of_cell(last - 1)
        gate(last, GATE_I, 1)
        gate(last, GATE_G, 1)
        hidden_state(last - 1)
        cell_state(last, 1)
        for part in range(2):
            gate(last, GATE_O, part)
            tanh_of_cell(last, part)
            hidden_state(last, part)
            store(last - 1 + part)
